import numpy as np
import ml_dtypes


def mxq(x, axis, fmt="e4m3"):
    dtype, down = {"e4m3": (ml_dtypes.float8_e4m3fn, 7), "e5m2": (ml_dtypes.float8_e5m2, 14)}[fmt]
    v = np.moveaxis(np.asarray(x, np.float32).astype(ml_dtypes.bfloat16).astype(np.float64), axis, -1)
    blocks = v.reshape(v.shape[:-1] + (-1, 32))
    amax = np.abs(blocks).max(-1, keepdims=True)
    byte = np.maximum(np.where(amax > 0, np.frexp(amax)[1] - 1 + 127, 0) - down, 1)
    scale = np.exp2(byte - 127.0)
    codes = (blocks / scale).astype(np.float32).astype(dtype).astype(np.float64)
    return np.moveaxis((codes * scale).reshape(v.shape), -1, axis)


WIDE = False


def mx_kscale(k):
    if not WIDE:
        return np.ones(k)
    levels = np.array([10, -10, 5, -5, 0])
    a = np.random.permutation(np.resize(levels, k // 512 * 4)).reshape(k // 512, 4)
    idx = np.arange(k)
    return np.exp2(a[idx // 512, idx % 128 // 32])


BF16 = ml_dtypes.bfloat16


def bf(x):
    return np.asarray(x, np.float32).astype(BF16)


def f64(x):
    return np.asarray(x).astype(np.float64)


B, S, D, E, H = 8, 1024, 256, 512, 8
HD = E // H


def setup_inputs():
    s = mx_kscale(E)
    f = np.tile(s.reshape(H, HD), (S // H, 1))[:, None, :]
    return {"h_attn": bf(np.random.standard_normal((B, S, H, HD)) * np.sqrt(np.e / H) * f),
            "Wo": bf(np.random.standard_normal((E, D)) / np.sqrt(E) / s[:, None]),
            "bo": bf(np.random.standard_normal(D) * 0.1)}


def reference(h_attn, Wo, bo):
    merged = f64(h_attn).transpose(0, 2, 1, 3).reshape(B, S, E)
    return (mxq(merged, 2, "e4m3") @ mxq(f64(Wo), 0, "e4m3")) + f64(bo)

@@ -1,0 +1,160 @@
+import concourse.mybir as mybir
+from concourse.masks import make_identity
+
+BF16 = mybir.dt.bfloat16
+F32 = mybir.dt.float32
+U32 = mybir.dt.uint32
+U8 = mybir.dt.uint8
+FP8X4 = mybir.dt.float8_e4m3fn_x4
+
+P = 128
+B, S, H, HD = 8, 1024, 8, 64
+E = H * HD
+D = 256
+J = E // HD
+ROWS = S // J
+HALVES = 2
+PACK = 4
+PAIR = 2
+UNIT_HEADS = 4
+UNITS_PER_BATCH = H // UNIT_HEADS
+UNITS = B * UNITS_PER_BATCH
+UNIT_PAIRS = UNIT_HEADS // PAIR
+HEADS_ON_VECTOR = 1
+FILL_UNITS = 2
+
+FLOPS = 2 * B * S * E * D
+
+
+def tile_multiheadrotaryattention_pb_t_kernel(tc, h_attn, Wo, bo, out):
+    nc = tc.nc
+    with tc.tile_pool(name="const", bufs=1) as const, tc.tile_pool(name="loads", bufs=B) as loads, tc.tile_pool(
+        name="work", bufs=4
+    ) as work, tc.psum_pool(name="flipped", bufs=4) as flipped, tc.psum_pool(
+        name="sums", bufs=4
+    ) as sums, tc.manual_schedule():
+        x_raw = []
+        for b in range(B):
+            raw = loads.tile([P, J * H * HD], BF16, tag="raw")
+            x_raw.append(raw)
+        w_raw = const.tile([P, PACK, D], BF16)
+        bias_row = const.tile([P, D], BF16)
+        nc.vector.memset(bias_row[:], 0.0)
+        for b in range(B):
+            nc.sync.dma_start(out=x_raw[b][:], in_=h_attn[b].rearrange("(p j) h d -> p (j h d)", j=J))
+            if b == 0:
+                nc.sync.dma_start(
+                    out=w_raw[:].rearrange("p (u e) c -> p u (e c)", u=HALVES),
+                    in_=Wo.rearrange("(u p e) c -> p u (e c)", u=HALVES, e=2),
+                )
+                nc.sync.dma_start(out=bias_row[0:1, :], in_=bo.rearrange("(o c) -> o c", o=1))
+
+        identity = const.tile([P, P], F32)
+        make_identity(nc, identity[:])
+        ones = const.tile([P, P], BF16)
+        nc.vector.memset(ones[:], 1.0)
+
+        w_grouped = const.tile([P, D, PACK], BF16, align_bytes=64)
+        w_codes = const.tile([P, D], U32, align_bytes=64)
+        w_scales = const.tile([P, D], U8, align_bytes=64)
+        bias_pair = const.tile([P, PAIR, D], F32)
+
+        def prepare_weights_and_bias():
+            nc.vector.tensor_copy(out=w_grouped[:], in_=w_raw[:].rearrange("p t c -> p c t"))
+            bias_sum = sums.tile([P, PAIR, D], F32, tag="acc")
+            nc.tensor.matmul(out=bias_sum[:, 0, :], lhsT=ones[:], rhs=bias_row[:], start=True, stop=True)
+            for q in range(PAIR):
+                nc.vector.tensor_copy(out=bias_pair[:, q, :], in_=bias_sum[:, 0, :])
+            nc.vector.quantize_mx(
+                out=w_codes[:].bitcast(FP8X4), scales=w_scales[:], in_=w_grouped[:].rearrange("p c t -> p (c t)")
+            )
+
+        x_head, x_grouped, x_codes, x_scales, x_sums = {}, {}, {}, {}, {}
+
+        def reorder(unit):
+            b, part = divmod(unit, UNITS_PER_BATCH)
+            first = part * UNIT_HEADS
+            nv = UNIT_HEADS if unit < FILL_UNITS else HEADS_ON_VECTOR
+            by_head = work.tile([P, UNIT_HEADS * J * HD], BF16, tag="by_head")
+            nc.vector.tensor_copy(
+                out=by_head[:].rearrange("p (h j d) -> p h j d", h=UNIT_HEADS, j=J)[:, 0:nv],
+                in_=x_raw[b][:].rearrange("p (j h d) -> p h j d", j=J, h=H)[:, first : first + nv],
+            )
+            if nv < UNIT_HEADS:
+                nc.scalar.copy(
+                    out=by_head[:].bitcast(F32).rearrange("p (h j w) -> p h j w", h=UNIT_HEADS, j=J)[:, nv:UNIT_HEADS],
+                    in_=x_raw[b][:]
+                    .bitcast(F32)
+                    .rearrange("p (j h w) -> p h j w", j=J, h=H)[:, first + nv : first + UNIT_HEADS],
+                )
+            x_head[unit] = by_head
+
+        def transpose(unit):
+            words = x_head[unit][:].bitcast(F32)
+            grouped = work.tile([P, UNIT_HEADS * ROWS * PACK], BF16, tag="grouped", align_bytes=64)
+            grouped_words = grouped[:].bitcast(F32)
+            for pair in range(UNIT_PAIRS):
+                bank = flipped.tile([P, PAIR * HALVES, ROWS], F32, tag="bank")
+                for q in range(PAIR * HALVES):
+                    first = (pair * PAIR * HALVES + q) * P
+                    nc.tensor.transpose(bank[:, q, :], words[:, first : first + P], identity[:])
+                width = PAIR * ROWS * HALVES
+                nc.scalar.copy(
+                    out=grouped_words[:, pair * width : (pair + 1) * width].rearrange(
+                        "p (h r u) -> p h r u", h=PAIR, u=HALVES
+                    ),
+                    in_=bank[:].rearrange("p (h u) r -> p h r u", h=PAIR),
+                )
+            x_grouped[unit] = grouped
+
+        def quantise(unit):
+            codes = work.tile([P, UNIT_HEADS * ROWS], U32, tag="codes", align_bytes=64)
+            scales = work.tile([P, UNIT_HEADS * ROWS], U8, tag="scales", align_bytes=64)
+            nc.vector.quantize_mx(out=codes[:].bitcast(FP8X4), scales=scales[:], in_=x_grouped[unit][:])
+            x_codes[unit] = codes
+            x_scales[unit] = scales
+
+        def multiply(unit):
+            x_sums[unit] = []
+            for pair in range(UNIT_PAIRS):
+                acc = sums.tile([P, PAIR, D], F32, tag="acc")
+                for q in range(PAIR):
+                    cols = slice((pair * PAIR + q) * ROWS, (pair * PAIR + q + 1) * ROWS)
+                    nc.tensor.matmul_mx(
+                        out=acc[:, q, :],
+                        lhsT=x_codes[unit][:, cols].bitcast(FP8X4),
+                        lhsT_scale=x_scales[unit][:, cols],
+                        rhs=w_codes[:].bitcast(FP8X4),
+                        rhs_scale=w_scales[:],
+                        start=True,
+                        stop=True,
+                    )
+                x_sums[unit].append(acc)
+
+        def add_bias_and_store(unit):
+            b, part = divmod(unit, UNITS_PER_BATCH)
+            result = work.tile([P, UNIT_HEADS, D], F32, tag="result")
+            for pair in range(UNIT_PAIRS):
+                nc.vector.tensor_tensor(
+                    out=result[:, pair * PAIR : (pair + 1) * PAIR, :],
+                    in0=x_sums[unit][pair][:],
+                    in1=bias_pair[:],
+                    op=mybir.AluOpType.add,
+                )
+            out_rows = out[b].rearrange("(h p) c -> p h c", p=ROWS)
+            nc.sync.dma_start(out=out_rows[:, part * UNIT_HEADS : (part + 1) * UNIT_HEADS, :], in_=result[:])
+
+        reorder(0)
+        reorder(1)
+        prepare_weights_and_bias()
+        transpose(0)
+        for unit in range(UNITS):
+            if unit + 2 < UNITS:
+                reorder(unit + 2)
+            if unit + 1 < UNITS:
+                transpose(unit + 1)
+            quantise(unit)
+            multiply(unit)
+            if unit >= 1:
+                add_bias_and_store(unit - 1)
+        add_bias_and_store(UNITS - 1)

@@ -30,7 +30,7 @@ def tile_multiheadrotaryattention_pb_t_kernel(tc, h_attn, Wo, bo, out):
     nc = tc.nc
     with tc.tile_pool(name="const", bufs=1) as const, tc.tile_pool(name="loads", bufs=B) as loads, tc.tile_pool(
         name="work", bufs=4
-    ) as work, tc.psum_pool(name="flipped", bufs=4) as flipped, tc.psum_pool(
+    ) as work, tc.tile_pool(name="results", bufs=UNITS) as results, tc.psum_pool(name="flipped", bufs=4) as flipped, tc.psum_pool(
         name="sums", bufs=4
     ) as sums, tc.manual_schedule():
         x_raw = []
@@ -133,7 +133,7 @@ def tile_multiheadrotaryattention_pb_t_kernel(tc, h_attn, Wo, bo, out):
 
         def add_bias_and_store(unit):
             b, part = divmod(unit, UNITS_PER_BATCH)
-            result = work.tile([P, UNIT_HEADS, D], F32, tag="result")
+            result = results.tile([P, UNIT_HEADS, D], F32, tag="result")
             for pair in range(UNIT_PAIRS):
                 nc.vector.tensor_tensor(
                     out=result[:, pair * PAIR : (pair + 1) * PAIR, :],

@@ -12,14 +12,15 @@ B, S, H, HD = 8, 1024, 8, 64
 E = H * HD
 D = 256
 J = E // HD
-ROWS = S // J
 HALVES = 2
 PACK = 4
+TWIN = 2
+GROUPS = B // TWIN
 PAIR = 2
 UNIT_HEADS = 4
-UNITS_PER_BATCH = H // UNIT_HEADS
-UNITS = B * UNITS_PER_BATCH
+HEAD_SETS = H // UNIT_HEADS
 UNIT_PAIRS = UNIT_HEADS // PAIR
+UNITS = GROUPS * HEAD_SETS * TWIN
 HEADS_ON_VECTOR = 1
 FILL_UNITS = 2
 
@@ -30,24 +31,31 @@ def tile_multiheadrotaryattention_pb_t_kernel(tc, h_attn, Wo, bo, out):
     nc = tc.nc
     with tc.tile_pool(name="const", bufs=1) as const, tc.tile_pool(name="loads", bufs=B) as loads, tc.tile_pool(
         name="work", bufs=4
-    ) as work, tc.tile_pool(name="results", bufs=UNITS) as results, tc.psum_pool(name="flipped", bufs=4) as flipped, tc.psum_pool(
-        name="sums", bufs=4
-    ) as sums, tc.manual_schedule():
-        x_raw = []
-        for b in range(B):
+    ) as work, tc.tile_pool(name="results", bufs=GROUPS * HEAD_SETS) as results, tc.psum_pool(
+        name="flipped", bufs=4
+    ) as flipped, tc.psum_pool(name="sums", bufs=4) as sums, tc.manual_schedule():
+        x_raw = {}
+
+        def load_rows(group, parity):
             raw = loads.tile([P, J * H * HD], BF16, tag="raw")
-            x_raw.append(raw)
+            for twin in range(TWIN):
+                tokens = h_attn[group * TWIN + twin].rearrange("(s a j) h d -> s a (j h d)", a=TWIN, j=J)
+                nc.sync.dma_start(out=raw[twin:P:TWIN, :], in_=tokens[:, parity, :])
+            x_raw[(group, parity)] = raw
+
         w_raw = const.tile([P, PACK, D], BF16)
         bias_row = const.tile([P, D], BF16)
         nc.vector.memset(bias_row[:], 0.0)
-        for b in range(B):
-            nc.sync.dma_start(out=x_raw[b][:], in_=h_attn[b].rearrange("(p j) h d -> p (j h d)", j=J))
-            if b == 0:
-                nc.sync.dma_start(
-                    out=w_raw[:].rearrange("p (u e) c -> p u (e c)", u=HALVES),
-                    in_=Wo.rearrange("(u p e) c -> p u (e c)", u=HALVES, e=2),
-                )
-                nc.sync.dma_start(out=bias_row[0:1, :], in_=bo.rearrange("(o c) -> o c", o=1))
+        load_rows(0, 0)
+        nc.sync.dma_start(
+            out=w_raw[:].rearrange("p (u e) c -> p u (e c)", u=HALVES),
+            in_=Wo.rearrange("(u p e) c -> p u (e c)", u=HALVES, e=2),
+        )
+        nc.sync.dma_start(out=bias_row[0:1, :], in_=bo.rearrange("(o c) -> o c", o=1))
+        load_rows(0, 1)
+        for group in range(1, GROUPS):
+            for parity in range(TWIN):
+                load_rows(group, parity)
 
         identity = const.tile([P, P], F32)
         make_identity(nc, identity[:])
@@ -69,36 +77,42 @@ def tile_multiheadrotaryattention_pb_t_kernel(tc, h_attn, Wo, bo, out):
                 out=w_codes[:].bitcast(FP8X4), scales=w_scales[:], in_=w_grouped[:].rearrange("p c t -> p (c t)")
             )
 
-        x_head, x_grouped, x_codes, x_scales, x_sums = {}, {}, {}, {}, {}
+        x_head, x_grouped, x_codes, x_scales, x_sums, x_result = {}, {}, {}, {}, {}, {}
+
+        def place(unit):
+            rest, parity = divmod(unit, TWIN)
+            group, head_set = divmod(rest, HEAD_SETS)
+            return group, head_set, parity
 
         def reorder(unit):
-            b, part = divmod(unit, UNITS_PER_BATCH)
-            first = part * UNIT_HEADS
+            group, head_set, parity = place(unit)
+            raw = x_raw[(group, parity)]
+            first = head_set * UNIT_HEADS
             nv = UNIT_HEADS if unit < FILL_UNITS else HEADS_ON_VECTOR
             by_head = work.tile([P, UNIT_HEADS * J * HD], BF16, tag="by_head")
             nc.vector.tensor_copy(
                 out=by_head[:].rearrange("p (h j d) -> p h j d", h=UNIT_HEADS, j=J)[:, 0:nv],
-                in_=x_raw[b][:].rearrange("p (j h d) -> p h j d", j=J, h=H)[:, first : first + nv],
+                in_=raw[:].rearrange("p (j h d) -> p h j d", j=J, h=H)[:, first : first + nv],
             )
             if nv < UNIT_HEADS:
                 nc.scalar.copy(
                     out=by_head[:].bitcast(F32).rearrange("p (h j w) -> p h j w", h=UNIT_HEADS, j=J)[:, nv:UNIT_HEADS],
-                    in_=x_raw[b][:]
-                    .bitcast(F32)
-                    .rearrange("p (j h w) -> p h j w", j=J, h=H)[:, first + nv : first + UNIT_HEADS],
+                    in_=raw[:].bitcast(F32).rearrange("p (j h w) -> p h j w", j=J, h=H)[
+                        :, first + nv : first + UNIT_HEADS
+                    ],
                 )
             x_head[unit] = by_head
 
         def transpose(unit):
             words = x_head[unit][:].bitcast(F32)
-            grouped = work.tile([P, UNIT_HEADS * ROWS * PACK], BF16, tag="grouped", align_bytes=64)
+            grouped = work.tile([P, UNIT_HEADS * P * PACK], BF16, tag="grouped", align_bytes=64)
             grouped_words = grouped[:].bitcast(F32)
             for pair in range(UNIT_PAIRS):
-                bank = flipped.tile([P, PAIR * HALVES, ROWS], F32, tag="bank")
+                bank = flipped.tile([P, PAIR * HALVES, P], F32, tag="bank")
                 for q in range(PAIR * HALVES):
                     first = (pair * PAIR * HALVES + q) * P
                     nc.tensor.transpose(bank[:, q, :], words[:, first : first + P], identity[:])
-                width = PAIR * ROWS * HALVES
+                width = PAIR * P * HALVES
                 nc.scalar.copy(
                     out=grouped_words[:, pair * width : (pair + 1) * width].rearrange(
                         "p (h r u) -> p h r u", h=PAIR, u=HALVES
@@ -108,8 +122,8 @@ def tile_multiheadrotaryattention_pb_t_kernel(tc, h_attn, Wo, bo, out):
             x_grouped[unit] = grouped
 
         def quantise(unit):
-            codes = work.tile([P, UNIT_HEADS * ROWS], U32, tag="codes", align_bytes=64)
-            scales = work.tile([P, UNIT_HEADS * ROWS], U8, tag="scales", align_bytes=64)
+            codes = work.tile([P, UNIT_HEADS * P], U32, tag="codes", align_bytes=64)
+            scales = work.tile([P, UNIT_HEADS * P], U8, tag="scales", align_bytes=64)
             nc.vector.quantize_mx(out=codes[:].bitcast(FP8X4), scales=scales[:], in_=x_grouped[unit][:])
             x_codes[unit] = codes
             x_scales[unit] = scales
@@ -119,7 +133,7 @@ def tile_multiheadrotaryattention_pb_t_kernel(tc, h_attn, Wo, bo, out):
             for pair in range(UNIT_PAIRS):
                 acc = sums.tile([P, PAIR, D], F32, tag="acc")
                 for q in range(PAIR):
-                    cols = slice((pair * PAIR + q) * ROWS, (pair * PAIR + q + 1) * ROWS)
+                    cols = slice((pair * PAIR + q) * P, (pair * PAIR + q + 1) * P)
                     nc.tensor.matmul_mx(
                         out=acc[:, q, :],
                         lhsT=x_codes[unit][:, cols].bitcast(FP8X4),
@@ -132,17 +146,24 @@ def tile_multiheadrotaryattention_pb_t_kernel(tc, h_attn, Wo, bo, out):
                 x_sums[unit].append(acc)
 
         def add_bias_and_store(unit):
-            b, part = divmod(unit, UNITS_PER_BATCH)
-            result = results.tile([P, UNIT_HEADS, D], F32, tag="result")
+            group, head_set, parity = place(unit)
+            if parity == 0:
+                result = results.tile([P, UNIT_HEADS, TWIN, D], F32, tag="result")
+                x_result[(group, head_set)] = result
+            result = x_result[(group, head_set)]
             for pair in range(UNIT_PAIRS):
+                heads = slice(pair * PAIR, (pair + 1) * PAIR)
                 nc.vector.tensor_tensor(
-                    out=result[:, pair * PAIR : (pair + 1) * PAIR, :],
-                    in0=x_sums[unit][pair][:],
-                    in1=bias_pair[:],
-                    op=mybir.AluOpType.add,
+                    out=result[:, heads, parity, :], in0=x_sums[unit][pair][:], in1=bias_pair[:], op=mybir.AluOpType.add
                 )
-            out_rows = out[b].rearrange("(h p) c -> p h c", p=ROWS)
-            nc.sync.dma_start(out=out_rows[:, part * UNIT_HEADS : (part + 1) * UNIT_HEADS, :], in_=result[:])
+                if parity == TWIN - 1:
+                    first = head_set * UNIT_HEADS + pair * PAIR
+                    for twin in range(TWIN):
+                        rows = out[group * TWIN + twin].rearrange("(h s a) c -> s h (a c)", h=H, a=TWIN)
+                        nc.sync.dma_start(
+                            out=rows[:, first : first + PAIR, :],
+                            in_=result[twin:P:TWIN, heads, :, :].rearrange("p h a c -> p h (a c)"),
+                        )
 
         reorder(0)
         reorder(1)

@@ -12,15 +12,15 @@ B, S, H, HD = 8, 1024, 8, 64
 E = H * HD
 D = 256
 J = E // HD
+ROWS = S // J
 HALVES = 2
 PACK = 4
-TWIN = 2
-GROUPS = B // TWIN
 PAIR = 2
+TWIN = 2
 UNIT_HEADS = 4
-HEAD_SETS = H // UNIT_HEADS
+UNITS_PER_BATCH = H // UNIT_HEADS
+UNITS = B * UNITS_PER_BATCH
 UNIT_PAIRS = UNIT_HEADS // PAIR
-UNITS = GROUPS * HEAD_SETS * TWIN
 HEADS_ON_VECTOR = 1
 FILL_UNITS = 2
 
@@ -31,34 +31,31 @@ def tile_multiheadrotaryattention_pb_t_kernel(tc, h_attn, Wo, bo, out):
     nc = tc.nc
     with tc.tile_pool(name="const", bufs=1) as const, tc.tile_pool(name="loads", bufs=B) as loads, tc.tile_pool(
         name="work", bufs=4
-    ) as work, tc.tile_pool(name="results", bufs=GROUPS * HEAD_SETS) as results, tc.psum_pool(
-        name="flipped", bufs=4
-    ) as flipped, tc.psum_pool(name="sums", bufs=4) as sums, tc.manual_schedule():
-        x_raw = {}
-
-        def load_rows(group, parity):
+    ) as work, tc.tile_pool(name="results", bufs=UNITS) as results, tc.psum_pool(name="flipped", bufs=4) as flipped, tc.psum_pool(
+        name="sums", bufs=4
+    ) as sums, tc.manual_schedule():
+        x_raw = []
+        for b in range(B):
             raw = loads.tile([P, J * H * HD], BF16, tag="raw")
-            for twin in range(TWIN):
-                tokens = h_attn[group * TWIN + twin].rearrange("(s a j) h d -> s a (j h d)", a=TWIN, j=J)
-                nc.sync.dma_start(out=raw[twin:P:TWIN, :], in_=tokens[:, parity, :])
-            x_raw[(group, parity)] = raw
-
+            x_raw.append(raw)
         w_raw = const.tile([P, PACK, D], BF16)
         bias_row = const.tile([P, D], BF16)
         nc.vector.memset(bias_row[:], 0.0)
-        load_rows(0, 0)
-        nc.sync.dma_start(
-            out=w_raw[:].rearrange("p (u e) c -> p u (e c)", u=HALVES),
-            in_=Wo.rearrange("(u p e) c -> p u (e c)", u=HALVES, e=2),
-        )
-        nc.sync.dma_start(out=bias_row[0:1, :], in_=bo.rearrange("(o c) -> o c", o=1))
-        load_rows(0, 1)
-        for group in range(1, GROUPS):
-            for parity in range(TWIN):
-                load_rows(group, parity)
+        for b in range(B):
+            nc.sync.dma_start(out=x_raw[b][:], in_=h_attn[b].rearrange("(p j) h d -> p (j h d)", j=J))
+            if b == 0:
+                nc.sync.dma_start(
+                    out=w_raw[:].rearrange("p (u e) c -> p u (e c)", u=HALVES),
+                    in_=Wo.rearrange("(u p e) c -> p u (e c)", u=HALVES, e=2),
+                )
+                nc.sync.dma_start(out=bias_row[0:1, :], in_=bo.rearrange("(o c) -> o c", o=1))
 
         identity = const.tile([P, P], F32)
         make_identity(nc, identity[:])
+        even_odd = const.tile([P, P], F32)
+        nc.vector.tensor_copy(
+            out=even_odd[:].rearrange("p (a s) -> p a s", a=TWIN), in_=identity[:].rearrange("p (s a) -> p a s", a=TWIN)
+        )
         ones = const.tile([P, P], BF16)
         nc.vector.memset(ones[:], 1.0)
 
@@ -77,53 +74,50 @@ def tile_multiheadrotaryattention_pb_t_kernel(tc, h_attn, Wo, bo, out):
                 out=w_codes[:].bitcast(FP8X4), scales=w_scales[:], in_=w_grouped[:].rearrange("p c t -> p (c t)")
             )
 
-        x_head, x_grouped, x_codes, x_scales, x_sums, x_result = {}, {}, {}, {}, {}, {}
-
-        def place(unit):
-            rest, parity = divmod(unit, TWIN)
-            group, head_set = divmod(rest, HEAD_SETS)
-            return group, head_set, parity
+        x_head, x_grouped, x_codes, x_scales, x_sums = {}, {}, {}, {}, {}
 
         def reorder(unit):
-            group, head_set, parity = place(unit)
-            raw = x_raw[(group, parity)]
-            first = head_set * UNIT_HEADS
+            b, part = divmod(unit, UNITS_PER_BATCH)
+            first = part * UNIT_HEADS
             nv = UNIT_HEADS if unit < FILL_UNITS else HEADS_ON_VECTOR
             by_head = work.tile([P, UNIT_HEADS * J * HD], BF16, tag="by_head")
             nc.vector.tensor_copy(
                 out=by_head[:].rearrange("p (h j d) -> p h j d", h=UNIT_HEADS, j=J)[:, 0:nv],
-                in_=raw[:].rearrange("p (j h d) -> p h j d", j=J, h=H)[:, first : first + nv],
+                in_=x_raw[b][:].rearrange("p (j h d) -> p h j d", j=J, h=H)[:, first : first + nv],
             )
             if nv < UNIT_HEADS:
                 nc.scalar.copy(
                     out=by_head[:].bitcast(F32).rearrange("p (h j w) -> p h j w", h=UNIT_HEADS, j=J)[:, nv:UNIT_HEADS],
-                    in_=raw[:].bitcast(F32).rearrange("p (j h w) -> p h j w", j=J, h=H)[
-                        :, first + nv : first + UNIT_HEADS
-                    ],
+                    in_=x_raw[b][:]
+                    .bitcast(F32)
+                    .rearrange("p (j h w) -> p h j w", j=J, h=H)[:, first + nv : first + UNIT_HEADS],
                 )
             x_head[unit] = by_head
 
         def transpose(unit):
             words = x_head[unit][:].bitcast(F32)
-            grouped = work.tile([P, UNIT_HEADS * P * PACK], BF16, tag="grouped", align_bytes=64)
+            grouped = work.tile([P, UNIT_HEADS * ROWS * PACK], BF16, tag="grouped", align_bytes=64)
             grouped_words = grouped[:].bitcast(F32)
             for pair in range(UNIT_PAIRS):
-                bank = flipped.tile([P, PAIR * HALVES, P], F32, tag="bank")
-                for q in range(PAIR * HALVES):
-                    first = (pair * PAIR * HALVES + q) * P
-                    nc.tensor.transpose(bank[:, q, :], words[:, first : first + P], identity[:])
-                width = PAIR * P * HALVES
+                bank = flipped.tile([P, HALVES, TWIN, PAIR, ROWS // TWIN], F32, tag="bank")
+                for h in range(PAIR):
+                    for u in range(HALVES):
+                        first = ((pair * PAIR + h) * HALVES + u) * P
+                        nc.tensor.transpose(
+                            bank[:, u, :, h, :],
+                            words[:, first : first + P],
+                            even_odd[:].rearrange("p (a s) -> p a s", a=TWIN),
+                        )
+                width = PAIR * ROWS * HALVES
                 nc.scalar.copy(
-                    out=grouped_words[:, pair * width : (pair + 1) * width].rearrange(
-                        "p (h r u) -> p h r u", h=PAIR, u=HALVES
-                    ),
-                    in_=bank[:].rearrange("p (h u) r -> p h r u", h=PAIR),
+                    out=grouped_words[:, pair * width : (pair + 1) * width].rearrange("p (c u) -> p c u", u=HALVES),
+                    in_=bank[:].rearrange("p u a h s -> p (a h s) u"),
                 )
             x_grouped[unit] = grouped
 
         def quantise(unit):
-            codes = work.tile([P, UNIT_HEADS * P], U32, tag="codes", align_bytes=64)
-            scales = work.tile([P, UNIT_HEADS * P], U8, tag="scales", align_bytes=64)
+            codes = work.tile([P, UNIT_HEADS * ROWS], U32, tag="codes", align_bytes=64)
+            scales = work.tile([P, UNIT_HEADS * ROWS], U8, tag="scales", align_bytes=64)
             nc.vector.quantize_mx(out=codes[:].bitcast(FP8X4), scales=scales[:], in_=x_grouped[unit][:])
             x_codes[unit] = codes
             x_scales[unit] = scales
@@ -133,7 +127,7 @@ def tile_multiheadrotaryattention_pb_t_kernel(tc, h_attn, Wo, bo, out):
             for pair in range(UNIT_PAIRS):
                 acc = sums.tile([P, PAIR, D], F32, tag="acc")
                 for q in range(PAIR):
-                    cols = slice((pair * PAIR + q) * P, (pair * PAIR + q + 1) * P)
+                    cols = slice((pair * PAIR + q) * ROWS, (pair * PAIR + q + 1) * ROWS)
                     nc.tensor.matmul_mx(
                         out=acc[:, q, :],
                         lhsT=x_codes[unit][:, cols].bitcast(FP8X4),
@@ -146,24 +140,20 @@ def tile_multiheadrotaryattention_pb_t_kernel(tc, h_attn, Wo, bo, out):
                 x_sums[unit].append(acc)
 
         def add_bias_and_store(unit):
-            group, head_set, parity = place(unit)
-            if parity == 0:
-                result = results.tile([P, UNIT_HEADS, TWIN, D], F32, tag="result")
-                x_result[(group, head_set)] = result
-            result = x_result[(group, head_set)]
+            b, part = divmod(unit, UNITS_PER_BATCH)
+            result = results.tile([P, UNIT_HEADS, D], F32, tag="result")
             for pair in range(UNIT_PAIRS):
-                heads = slice(pair * PAIR, (pair + 1) * PAIR)
                 nc.vector.tensor_tensor(
-                    out=result[:, heads, parity, :], in0=x_sums[unit][pair][:], in1=bias_pair[:], op=mybir.AluOpType.add
+                    out=result[:, pair * PAIR : (pair + 1) * PAIR, :],
+                    in0=x_sums[unit][pair][:],
+                    in1=bias_pair[:],
+                    op=mybir.AluOpType.add,
                 )
-                if parity == TWIN - 1:
-                    first = head_set * UNIT_HEADS + pair * PAIR
-                    for twin in range(TWIN):
-                        rows = out[group * TWIN + twin].rearrange("(h s a) c -> s h (a c)", h=H, a=TWIN)
-                        nc.sync.dma_start(
-                            out=rows[:, first : first + PAIR, :],
-                            in_=result[twin:P:TWIN, heads, :, :].rearrange("p h a c -> p h (a c)"),
-                        )
+            out_rows = out[b].rearrange("(g m a) c -> m g (a c)", m=P, a=TWIN)
+            nc.sync.dma_start(
+                out=out_rows[:, part * UNIT_PAIRS : (part + 1) * UNIT_PAIRS, :],
+                in_=result[:].rearrange("p (g a) c -> p g (a c)", a=TWIN),
+            )
 
         reorder(0)
         reorder(1)

import concourse.mybir as mybir
from concourse.masks import make_identity

BF16 = mybir.dt.bfloat16
F32 = mybir.dt.float32
U32 = mybir.dt.uint32
U8 = mybir.dt.uint8
FP8X4 = mybir.dt.float8_e4m3fn_x4

P = 128
B, S, H, HD = 8, 1024, 8, 64
E = H * HD
D = 256
J = E // HD
ROWS = S // J
HALVES = 2
PACK = 4
PAIR = 2
TWIN = 2
UNIT_HEADS = 4
UNITS_PER_BATCH = H // UNIT_HEADS
UNITS = B * UNITS_PER_BATCH
UNIT_PAIRS = UNIT_HEADS // PAIR
HEADS_ON_VECTOR = 1
FILL_UNITS = 2

FLOPS = 2 * B * S * E * D


def tile_multiheadrotaryattention_pb_t_kernel(tc, h_attn, Wo, bo, out):
    nc = tc.nc
    with tc.tile_pool(name="const", bufs=1) as const, tc.tile_pool(name="loads", bufs=B) as loads, tc.tile_pool(
        name="work", bufs=4
    ) as work, tc.tile_pool(name="results", bufs=UNITS) as results, tc.psum_pool(name="flipped", bufs=4) as flipped, tc.psum_pool(
        name="sums", bufs=4
    ) as sums, tc.manual_schedule():
        x_raw = []
        for b in range(B):
            raw = loads.tile([P, J * H * HD], BF16, tag="raw")
            x_raw.append(raw)
        w_raw = const.tile([P, PACK, D], BF16)
        bias_row = const.tile([P, D], BF16)
        nc.vector.memset(bias_row[:], 0.0)
        for b in range(B):
            nc.sync.dma_start(out=x_raw[b][:], in_=h_attn[b].rearrange("(p j) h d -> p (j h d)", j=J))
            if b == 0:
                nc.sync.dma_start(
                    out=w_raw[:].rearrange("p (u e) c -> p u (e c)", u=HALVES),
                    in_=Wo.rearrange("(u p e) c -> p u (e c)", u=HALVES, e=2),
                )
                nc.sync.dma_start(out=bias_row[0:1, :], in_=bo.rearrange("(o c) -> o c", o=1))

        identity = const.tile([P, P], F32)
        make_identity(nc, identity[:])
        even_odd = const.tile([P, P], F32)
        nc.vector.tensor_copy(
            out=even_odd[:].rearrange("p (a s) -> p a s", a=TWIN), in_=identity[:].rearrange("p (s a) -> p a s", a=TWIN)
        )
        ones = const.tile([P, P], BF16)
        nc.vector.memset(ones[:], 1.0)

        w_grouped = const.tile([P, D, PACK], BF16, align_bytes=64)
        w_codes = const.tile([P, D], U32, align_bytes=64)
        w_scales = const.tile([P, D], U8, align_bytes=64)
        bias_pair = const.tile([P, PAIR, D], F32)

        def prepare_weights_and_bias():
            nc.vector.tensor_copy(out=w_grouped[:], in_=w_raw[:].rearrange("p t c -> p c t"))
            bias_sum = sums.tile([P, PAIR, D], F32, tag="acc")
            nc.tensor.matmul(out=bias_sum[:, 0, :], lhsT=ones[:], rhs=bias_row[:], start=True, stop=True)
            for q in range(PAIR):
                nc.vector.tensor_copy(out=bias_pair[:, q, :], in_=bias_sum[:, 0, :])
            nc.vector.quantize_mx(
                out=w_codes[:].bitcast(FP8X4), scales=w_scales[:], in_=w_grouped[:].rearrange("p c t -> p (c t)")
            )

        x_head, x_grouped, x_codes, x_scales, x_sums = {}, {}, {}, {}, {}

        def reorder(unit):
            b, part = divmod(unit, UNITS_PER_BATCH)
            first = part * UNIT_HEADS
            nv = UNIT_HEADS if unit < FILL_UNITS else HEADS_ON_VECTOR
            by_head = work.tile([P, UNIT_HEADS * J * HD], BF16, tag="by_head")
            nc.vector.tensor_copy(
                out=by_head[:].rearrange("p (h j d) -> p h j d", h=UNIT_HEADS, j=J)[:, 0:nv],
                in_=x_raw[b][:].rearrange("p (j h d) -> p h j d", j=J, h=H)[:, first : first + nv],
            )
            if nv < UNIT_HEADS:
                nc.scalar.copy(
                    out=by_head[:].bitcast(F32).rearrange("p (h j w) -> p h j w", h=UNIT_HEADS, j=J)[:, nv:UNIT_HEADS],
                    in_=x_raw[b][:]
                    .bitcast(F32)
                    .rearrange("p (j h w) -> p h j w", j=J, h=H)[:, first + nv : first + UNIT_HEADS],
                )
            x_head[unit] = by_head

        def transpose(unit):
            words = x_head[unit][:].bitcast(F32)
            grouped = work.tile([P, UNIT_HEADS * ROWS * PACK], BF16, tag="grouped", align_bytes=64)
            grouped_words = grouped[:].bitcast(F32)
            for pair in range(UNIT_PAIRS):
                bank = flipped.tile([P, HALVES, TWIN, PAIR, ROWS // TWIN], F32, tag="bank")
                for h in range(PAIR):
                    for u in range(HALVES):
                        first = ((pair * PAIR + h) * HALVES + u) * P
                        nc.tensor.transpose(
                            bank[:, u, :, h, :],
                            words[:, first : first + P],
                            even_odd[:].rearrange("p (a s) -> p a s", a=TWIN),
                        )
                width = PAIR * ROWS * HALVES
                nc.scalar.copy(
                    out=grouped_words[:, pair * width : (pair + 1) * width].rearrange("p (c u) -> p c u", u=HALVES),
                    in_=bank[:].rearrange("p u a h s -> p (a h s) u"),
                )
            x_grouped[unit] = grouped

        def quantise(unit):
            codes = work.tile([P, UNIT_HEADS * ROWS], U32, tag="codes", align_bytes=64)
            scales = work.tile([P, UNIT_HEADS * ROWS], U8, tag="scales", align_bytes=64)
            nc.vector.quantize_mx(out=codes[:].bitcast(FP8X4), scales=scales[:], in_=x_grouped[unit][:])
            x_codes[unit] = codes
            x_scales[unit] = scales

        def multiply(unit):
            x_sums[unit] = []
            for pair in range(UNIT_PAIRS):
                acc = sums.tile([P, PAIR, D], F32, tag="acc")
                for q in range(PAIR):
                    cols = slice((pair * PAIR + q) * ROWS, (pair * PAIR + q + 1) * ROWS)
                    nc.tensor.matmul_mx(
                        out=acc[:, q, :],
                        lhsT=x_codes[unit][:, cols].bitcast(FP8X4),
                        lhsT_scale=x_scales[unit][:, cols],
                        rhs=w_codes[:].bitcast(FP8X4),
                        rhs_scale=w_scales[:],
                        start=True,
                        stop=True,
                    )
                x_sums[unit].append(acc)

        def add_bias_and_store(unit):
            b, part = divmod(unit, UNITS_PER_BATCH)
            result = results.tile([P, UNIT_HEADS, D], F32, tag="result")
            for pair in range(UNIT_PAIRS):
                nc.vector.tensor_tensor(
                    out=result[:, pair * PAIR : (pair + 1) * PAIR, :],
                    in0=x_sums[unit][pair][:],
                    in1=bias_pair[:],
                    op=mybir.AluOpType.add,
                )
            out_rows = out[b].rearrange("(g m a) c -> m g (a c)", m=P, a=TWIN)
            nc.sync.dma_start(
                out=out_rows[:, part * UNIT_PAIRS : (part + 1) * UNIT_PAIRS, :],
                in_=result[:].rearrange("p (g a) c -> p g (a c)", a=TWIN),
            )

        reorder(0)
        reorder(1)
        prepare_weights_and_bias()
        transpose(0)
        for unit in range(UNITS):
            if unit + 2 < UNITS:
                reorder(unit + 2)
            if unit + 1 < UNITS:
                transpose(unit + 1)
            quantise(unit)
            multiply(unit)
            if unit >= 1:
                add_bias_and_store(unit - 1)
        add_bias_and_store(UNITS - 1)
